import numpy as np
import ml_dtypes


def mxq(x, axis, fmt="e4m3"):
    dtype, down = {"e4m3": (ml_dtypes.float8_e4m3fn, 7), "e5m2": (ml_dtypes.float8_e5m2, 14)}[fmt]
    v = np.moveaxis(np.asarray(x, np.float32).astype(ml_dtypes.bfloat16).astype(np.float64), axis, -1)
    blocks = v.reshape(v.shape[:-1] + (-1, 32))
    amax = np.abs(blocks).max(-1, keepdims=True)
    byte = np.maximum(np.where(amax > 0, np.frexp(amax)[1] - 1 + 127, 0) - down, 1)
    scale = np.exp2(byte - 127.0)
    codes = (blocks / scale).astype(np.float32).astype(dtype).astype(np.float64)
    return np.moveaxis((codes * scale).reshape(v.shape), -1, axis)


WIDE = False


def mx_kscale(k):
    if not WIDE:
        return np.ones(k)
    levels = np.array([10, -10, 5, -5, 0])
    a = np.random.permutation(np.resize(levels, k // 512 * 4)).reshape(k // 512, 4)
    idx = np.arange(k)
    return np.exp2(a[idx // 512, idx % 128 // 32])


BF16 = ml_dtypes.bfloat16


def bf(x):
    return np.asarray(x, np.float32).astype(BF16)


def f64(x):
    return np.asarray(x).astype(np.float64)


E2M1 = np.array([0.0, 0.5, 1.0, 1.5, 2.0, 3.0, 4.0, 6.0, -0.0, -0.5, -1.0, -1.5, -2.0, -3.0, -4.0, -6.0])


def pack_weight(w, fmt):
    k, n = w.shape
    w = f64(bf(w)).reshape(k // 32, 32, n)
    amax = np.abs(w).max(1)
    if fmt == "e4m3":
        byte = np.frexp(amax)[1] - 1 + 127 - 7
    else:
        mant, ex = np.frexp(amax / 6.0)
        byte = np.where(mant > 0.5, ex, ex - 1) + 127
    byte = np.clip(np.where(amax > 0, byte, 1), 1, 254)
    scaled = (w * np.exp2(127.0 - byte)[:, None, :]).reshape(k, n).astype(np.float32)
    by_word = np.ascontiguousarray(scaled.reshape(k // 512, 128, 4, n).transpose(0, 1, 3, 2))
    if fmt == "e4m3":
        words = by_word.astype(ml_dtypes.float8_e4m3fn).view(np.uint8)
    else:
        c = by_word.astype(ml_dtypes.float4_e2m1fn).view(np.uint8) & 0xF
        words = c[..., 0::2] | (c[..., 1::2] << 4)
    return np.ascontiguousarray(words), np.ascontiguousarray(byte.astype(np.uint8).reshape(k // 512, 16, n))


def unpack_weight(words, scales, fmt):
    g, p, n, _ = words.shape
    if fmt == "e4m3":
        vals = np.ascontiguousarray(words).view(ml_dtypes.float8_e4m3fn).astype(np.float64)
    else:
        nib = np.empty((g, p, n, 4), np.uint8)
        nib[..., 0::2] = words & 0xF
        nib[..., 1::2] = words >> 4
        vals = E2M1[nib]
    vals = vals * np.repeat(np.exp2(scales.astype(np.float64) - 127.0), 8, axis=1)[..., None]
    return vals.transpose(0, 1, 3, 2).reshape(g * 512, n)


B, K, N = 2048, 512, 1024
NACT = 4


def setup_inputs():
    s = mx_kscale(K)
    g = np.tile(np.array([1.0, 1.0, 1.0, 0.5]), N // NACT)
    x = np.random.standard_normal((B, K)) * s
    weight = np.random.uniform(-1.0, 1.0, (N, K)) / np.sqrt(K) * g[:, None] / s[None, :]
    words, scales = pack_weight(weight.T, "e4m3")
    return {"x": bf(x), "weight_words": words, "weight_scales": scales}


def reference(x, weight_words, weight_scales):
    y = mxq(f64(x), 1, "e4m3") @ unpack_weight(weight_words, weight_scales, "e4m3")
    rows, cols = y.shape
    y3 = y.reshape(rows, cols // NACT, NACT)
    out = np.stack(
        [y3[..., 0],
         np.cos(y3[..., 1]),
         np.sin(y3[..., 2]),
         np.tan(y3[..., 3])],
        axis=-1,
    )
    return out.reshape(rows, cols)

@@ -1,0 +1,216 @@
+import math
+from contextlib import ExitStack
+
+import concourse.mybir as mybir
+from concourse.masks import make_identity
+
+F32 = mybir.dt.float32
+BF16 = mybir.dt.bfloat16
+I32 = mybir.dt.int32
+U32 = mybir.dt.uint32
+U8 = mybir.dt.uint8
+FP8X4 = mybir.dt.float8_e4m3fn_x4
+FUNC = mybir.ActivationFunctionType
+ALU = mybir.AluOpType
+
+P = 128
+ROWS, K, N = 2048, 512, 1024
+FLOPS = 2 * ROWS * K * N
+
+TILES = ROWS // P
+BANK = 512
+HALVES = N // BANK
+CLASSES = 4
+LINEAR, COS, SIN, TAN = 0, 1, 2, 3
+PER_BANK = BANK // CLASSES
+PER_TILE = N // CLASSES
+WORDS = K // 2
+
+PAIR = 2
+PAIRS = TILES // PAIR
+GROUPS = 2
+GROUP_PAIRS = PAIRS // GROUPS
+
+TWO_PI = 2.0 * math.pi
+
+
+def tile_mylayerfunc_kernel(tc, x, weight_words, weight_scales, out):
+    nc = tc.nc
+    with ExitStack() as ctx:
+        keep = ctx.enter_context(tc.tile_pool(name="keep", bufs=1))
+        work = ctx.enter_context(tc.tile_pool(name="work", bufs=4))
+        psum_x = ctx.enter_context(tc.psum_pool(name="psum_x", bufs=2))
+        psum_y = ctx.enter_context(tc.psum_pool(name="psum_y", bufs=6))
+
+        x_view = x.rearrange("(p t) k -> p t k", t=TILES)
+        out_view = out.rearrange("(p t) n -> p t n", t=TILES)
+
+        ident = keep.tile([P, P], F32)
+        make_identity(nc, ident[:])
+
+        x_sb = keep.tile([P, TILES, K], BF16)
+        grouped = keep.tile([P, TILES, P, 2], F32, align_bytes=64)
+        x_codes = keep.tile([P, TILES * P], U32, align_bytes=64)
+        x_scales = keep.tile([P, TILES * P], U8, align_bytes=64)
+        w_codes = keep.tile([P, N], U32, align_bytes=64)
+        w_scales = keep.tile([P, N], U8, align_bytes=64)
+        planes = keep.tile([P, TILES, CLASSES, PER_TILE], F32)
+        secant = keep.tile([P, TILES, PER_TILE], F32)
+        tan_turns = keep.tile([P, PAIR * HALVES, PER_BANK], I32)
+        turns = keep.tile([P, HALVES, TAN, PER_BANK], I32)
+        shifts = keep.tile([P, 2, 1], F32)
+
+        def stage_x(pair):
+            xt = psum_x.tile([P, PAIR, 2, P], F32)
+            for i in range(PAIR):
+                words = x_sb[:, pair * PAIR + i, :].bitcast(F32)
+                for u in range(2):
+                    nc.tensor.transpose(xt[:, i, u, :], words[:, u:WORDS:2], ident[:])
+            nc.scalar.copy(
+                out=grouped[:, pair * PAIR : (pair + 1) * PAIR, :, :],
+                in_=xt[:].rearrange("p i u r -> p i r u"),
+            )
+
+        def quantise(pair):
+            tiles = slice(pair * PAIR, (pair + 1) * PAIR)
+            cols = slice(pair * PAIR * P, (pair + 1) * PAIR * P)
+            nc.vector.quantize_mx(
+                out=x_codes[:, cols].bitcast(FP8X4),
+                scales=x_scales[:, cols],
+                in_=grouped[:, tiles, :, :].rearrange("p t r u -> p (t r u)").bitcast(BF16),
+            )
+
+        def product(t, h):
+            y = psum_y.tile([P, BANK], F32)
+            nc.tensor.matmul_mx(
+                out=y[:],
+                lhsT=x_codes[:, t * P : (t + 1) * P].bitcast(FP8X4),
+                lhsT_scale=x_scales[:, t * P : (t + 1) * P],
+                rhs=w_codes[:, h * BANK : (h + 1) * BANK].bitcast(FP8X4),
+                rhs_scale=w_scales[:, h * BANK : (h + 1) * BANK],
+                start=True,
+                stop=True,
+            )
+            return y[:].rearrange("p (c a) -> p a c", a=CLASSES)
+
+
+        def tan_angles(pair):
+            banks = [(pair * PAIR + i, h) for i in range(PAIR) for h in range(HALVES)]
+            ys = [product(t, h) for t, h in banks]
+            for b, y in enumerate(ys):
+                nc.vector.tensor_scalar(
+                    out=tan_turns[:, b, :],
+                    in0=y[:, TAN, :],
+                    scalar1=1.0 / math.pi,
+                    scalar2=0.0,
+                    op0=ALU.mult,
+                    op1=ALU.add,
+                )
+            for b, y in enumerate(ys):
+                t, h = banks[b]
+                nc.vector.scalar_tensor_tensor(
+                    out=planes[:, t, TAN, h * PER_BANK : (h + 1) * PER_BANK],
+                    in0=tan_turns[:, b, :],
+                    scalar=-math.pi,
+                    in1=y[:, TAN, :],
+                    op0=ALU.mult,
+                    op1=ALU.add,
+                )
+
+        def tan_sine(pair):
+            tiles = slice(pair * PAIR, (pair + 1) * PAIR)
+            nc.scalar.activation(out=planes[:, tiles, TAN, :], in_=planes[:, tiles, TAN, :], func=FUNC.Sin)
+
+        def tan_square(pair):
+            tiles = slice(pair * PAIR, (pair + 1) * PAIR)
+            nc.scalar.activation(out=secant[:, tiles, :], in_=planes[:, tiles, TAN, :], func=FUNC.Square)
+
+        def tan_finish(pair):
+            tiles = slice(pair * PAIR, (pair + 1) * PAIR)
+            nc.scalar.activation(
+                out=secant[:, tiles, :], in_=secant[:, tiles, :], func=FUNC.Abs_reciprocal_sqrt, bias=1.0, scale=-1.0
+            )
+            nc.gpsimd.tensor_tensor(
+                out=planes[:, tiles, TAN, :], in0=planes[:, tiles, TAN, :], in1=secant[:, tiles, :], op=ALU.mult
+            )
+
+        def main_angles(t):
+            ys = [product(t, h) for h in range(HALVES)]
+            for h, y in enumerate(ys):
+                nc.vector.scalar_tensor_tensor(
+                    out=turns[:, h, COS:TAN, :],
+                    in0=y[:, COS:TAN, :],
+                    scalar=1.0 / TWO_PI,
+                    in1=shifts[:].to_broadcast([P, 2, PER_BANK]),
+                    op0=ALU.mult,
+                    op1=ALU.add,
+                )
+            for h, y in enumerate(ys):
+                nc.vector.scalar_tensor_tensor(
+                    out=planes[:, t, LINEAR:TAN, h * PER_BANK : (h + 1) * PER_BANK],
+                    in0=turns[:, h, :, :],
+                    scalar=-TWO_PI,
+                    in1=y[:, LINEAR:TAN, :],
+                    op0=ALU.mult,
+                    op1=ALU.add,
+                )
+
+        def main_finish(t):
+            nc.scalar.activation(
+                out=planes[:, t, COS, :], in_=planes[:, t, COS, :], func=FUNC.Sin, bias=0.5 * math.pi
+            )
+            nc.scalar.activation(out=planes[:, t, SIN, :], in_=planes[:, t, SIN, :], func=FUNC.Sin)
+            result = work.tile([P, PER_TILE, CLASSES], F32)
+            nc.gpsimd.tensor_scalar(
+                out=result[:],
+                in0=planes[:, t, :, :].rearrange("p a j -> p j a"),
+                scalar1=1.0,
+                scalar2=0.0,
+                op0=ALU.mult,
+                op1=ALU.add,
+            )
+            nc.sync.dma_start(out=out_view[:, t, :], in_=result[:].rearrange("p j a -> p (j a)"))
+
+        def load_x(pair):
+            tiles = slice(pair * PAIR, (pair + 1) * PAIR)
+            nc.sync.dma_start(out=x_sb[:, tiles, :], in_=x_view[:, tiles, :])
+
+        with tc.manual_schedule():
+            nc.vector.memset(w_scales[:].bitcast(I32), 0)
+            nc.vector.memset(turns[:, :, LINEAR, :], 0)
+            nc.vector.memset(shifts[:, 0, :], 0.25)
+            nc.vector.memset(shifts[:, 1, :], 0.0)
+            load_x(0)
+            load_x(1)
+            for quadrant in range(4):
+                nc.sync.dma_start(
+                    out=w_scales[32 * quadrant : 32 * quadrant + 4, :].bitcast(I32),
+                    in_=weight_scales[0, 4 * quadrant : 4 * quadrant + 4, :].bitcast(I32),
+                )
+            nc.sync.dma_start(
+                out=w_codes[:].bitcast(I32),
+                in_=weight_words[0].rearrange("p n t -> p (n t)").bitcast(I32),
+            )
+            for pair in range(2, PAIRS):
+                load_x(pair)
+
+            stage_x(0)
+            stage_x(1)
+            quantise(0)
+            for group in range(GROUPS):
+                pairs = range(group * GROUP_PAIRS, (group + 1) * GROUP_PAIRS)
+                for pair in pairs:
+                    if pair + 2 < PAIRS:
+                        stage_x(pair + 2)
+                    if pair + 1 < PAIRS:
+                        quantise(pair + 1)
+                    tan_angles(pair)
+                    tan_sine(pair)
+                    if pair > pairs[0]:
+                        tan_square(pair - 1)
+                tan_square(pairs[-1])
+                for pair in pairs:
+                    tan_finish(pair)
+                for t in range(pairs[0] * PAIR, (pairs[-1] + 1) * PAIR):
+                    main_angles(t)
+                    main_finish(t)

@@ -30,6 +30,8 @@ PAIR = 2
 PAIRS = TILES // PAIR
 GROUPS = 2
 GROUP_PAIRS = PAIRS // GROUPS
+GROUP_TILES = TILES // GROUPS
+LAG = 5
 
 TWO_PI = 2.0 * math.pi
 
@@ -125,17 +127,13 @@ def tile_mylayerfunc_kernel(tc, x, weight_words, weight_scales, out):
             tiles = slice(pair * PAIR, (pair + 1) * PAIR)
             nc.scalar.activation(out=secant[:, tiles, :], in_=planes[:, tiles, TAN, :], func=FUNC.Square)
 
-        def tan_finish(pair):
+        def tan_secant(pair):
             tiles = slice(pair * PAIR, (pair + 1) * PAIR)
             nc.scalar.activation(
                 out=secant[:, tiles, :], in_=secant[:, tiles, :], func=FUNC.Abs_reciprocal_sqrt, bias=1.0, scale=-1.0
             )
-            nc.gpsimd.tensor_tensor(
-                out=planes[:, tiles, TAN, :], in0=planes[:, tiles, TAN, :], in1=secant[:, tiles, :], op=ALU.mult
-            )
 
-        def main_angles(t):
-            ys = [product(t, h) for h in range(HALVES)]
+        def count_turns(ys):
             for h, y in enumerate(ys):
                 nc.vector.scalar_tensor_tensor(
                     out=turns[:, h, COS:TAN, :],
@@ -145,6 +143,8 @@ def tile_mylayerfunc_kernel(tc, x, weight_words, weight_scales, out):
                     op0=ALU.mult,
                     op1=ALU.add,
                 )
+
+        def take_turns_off(t, ys):
             for h, y in enumerate(ys):
                 nc.vector.scalar_tensor_tensor(
                     out=planes[:, t, LINEAR:TAN, h * PER_BANK : (h + 1) * PER_BANK],
@@ -155,20 +155,20 @@ def tile_mylayerfunc_kernel(tc, x, weight_words, weight_scales, out):
                     op1=ALU.add,
                 )
 
-        def main_finish(t):
+        def sines(t):
             nc.scalar.activation(
                 out=planes[:, t, COS, :], in_=planes[:, t, COS, :], func=FUNC.Sin, bias=0.5 * math.pi
             )
             nc.scalar.activation(out=planes[:, t, SIN, :], in_=planes[:, t, SIN, :], func=FUNC.Sin)
-            result = work.tile([P, PER_TILE, CLASSES], F32)
-            nc.gpsimd.tensor_scalar(
-                out=result[:],
-                in0=planes[:, t, :, :].rearrange("p a j -> p j a"),
-                scalar1=1.0,
-                scalar2=0.0,
-                op0=ALU.mult,
-                op1=ALU.add,
+
+        def tan_product(t):
+            nc.vector.tensor_tensor(
+                out=planes[:, t, TAN, :], in0=planes[:, t, TAN, :], in1=secant[:, t, :], op=ALU.mult
             )
+
+        def interleave_and_store(t):
+            result = work.tile([P, PER_TILE, CLASSES], F32)
+            nc.vector.tensor_copy(out=result[:], in_=planes[:, t, :, :].rearrange("p a j -> p j a"))
             nc.sync.dma_start(out=out_view[:, t, :], in_=result[:].rearrange("p j a -> p (j a)"))
 
         def load_x(pair):
@@ -210,7 +210,19 @@ def tile_mylayerfunc_kernel(tc, x, weight_words, weight_scales, out):
                         tan_square(pair - 1)
                 tan_square(pairs[-1])
                 for pair in pairs:
-                    tan_finish(pair)
-                for t in range(pairs[0] * PAIR, (pairs[-1] + 1) * PAIR):
-                    main_angles(t)
-                    main_finish(t)
+                    tan_secant(pair)
+                tiles = range(group * GROUP_TILES, (group + 1) * GROUP_TILES)
+                for t in tiles:
+                    due = t - LAG
+                    ys = [product(t, h) for h in range(HALVES)]
+                    count_turns(ys)
+                    if due >= tiles[0]:
+                        tan_product(due)
+                    take_turns_off(t, ys)
+                    sines(t)
+                    if due >= tiles[0]:
+                        interleave_and_store(due)
+                for due in tiles[-LAG:]:
+                    tan_product(due)
+                for due in tiles[-LAG:]:
+                    interleave_and_store(due)

@@ -30,8 +30,6 @@ PAIR = 2
 PAIRS = TILES // PAIR
 GROUPS = 2
 GROUP_PAIRS = PAIRS // GROUPS
-GROUP_TILES = TILES // GROUPS
-LAG = 5
 
 TWO_PI = 2.0 * math.pi
 
@@ -127,13 +125,17 @@ def tile_mylayerfunc_kernel(tc, x, weight_words, weight_scales, out):
             tiles = slice(pair * PAIR, (pair + 1) * PAIR)
             nc.scalar.activation(out=secant[:, tiles, :], in_=planes[:, tiles, TAN, :], func=FUNC.Square)
 
-        def tan_secant(pair):
+        def tan_finish(pair):
             tiles = slice(pair * PAIR, (pair + 1) * PAIR)
             nc.scalar.activation(
                 out=secant[:, tiles, :], in_=secant[:, tiles, :], func=FUNC.Abs_reciprocal_sqrt, bias=1.0, scale=-1.0
             )
+            nc.gpsimd.tensor_tensor(
+                out=planes[:, tiles, TAN, :], in0=planes[:, tiles, TAN, :], in1=secant[:, tiles, :], op=ALU.mult
+            )
 
-        def count_turns(ys):
+        def main_angles(t):
+            ys = [product(t, h) for h in range(HALVES)]
             for h, y in enumerate(ys):
                 nc.vector.scalar_tensor_tensor(
                     out=turns[:, h, COS:TAN, :],
@@ -143,8 +145,6 @@ def tile_mylayerfunc_kernel(tc, x, weight_words, weight_scales, out):
                     op0=ALU.mult,
                     op1=ALU.add,
                 )
-
-        def take_turns_off(t, ys):
             for h, y in enumerate(ys):
                 nc.vector.scalar_tensor_tensor(
                     out=planes[:, t, LINEAR:TAN, h * PER_BANK : (h + 1) * PER_BANK],
@@ -155,20 +155,20 @@ def tile_mylayerfunc_kernel(tc, x, weight_words, weight_scales, out):
                     op1=ALU.add,
                 )
 
-        def sines(t):
+        def main_finish(t):
             nc.scalar.activation(
                 out=planes[:, t, COS, :], in_=planes[:, t, COS, :], func=FUNC.Sin, bias=0.5 * math.pi
             )
             nc.scalar.activation(out=planes[:, t, SIN, :], in_=planes[:, t, SIN, :], func=FUNC.Sin)
-
-        def tan_product(t):
-            nc.vector.tensor_tensor(
-                out=planes[:, t, TAN, :], in0=planes[:, t, TAN, :], in1=secant[:, t, :], op=ALU.mult
-            )
-
-        def interleave_and_store(t):
             result = work.tile([P, PER_TILE, CLASSES], F32)
-            nc.vector.tensor_copy(out=result[:], in_=planes[:, t, :, :].rearrange("p a j -> p j a"))
+            nc.gpsimd.tensor_scalar(
+                out=result[:],
+                in0=planes[:, t, :, :].rearrange("p a j -> p j a"),
+                scalar1=1.0,
+                scalar2=0.0,
+                op0=ALU.mult,
+                op1=ALU.add,
+            )
             nc.sync.dma_start(out=out_view[:, t, :], in_=result[:].rearrange("p j a -> p (j a)"))
 
         def load_x(pair):
@@ -180,8 +180,8 @@ def tile_mylayerfunc_kernel(tc, x, weight_words, weight_scales, out):
             nc.vector.memset(turns[:, :, LINEAR, :], 0)
             nc.vector.memset(shifts[:, 0, :], 0.25)
             nc.vector.memset(shifts[:, 1, :], 0.0)
-            load_x(0)
-            load_x(1)
+            for pair in range(4):
+                load_x(pair)
             for quadrant in range(4):
                 nc.sync.dma_start(
                     out=w_scales[32 * quadrant : 32 * quadrant + 4, :].bitcast(I32),
@@ -191,38 +191,27 @@ def tile_mylayerfunc_kernel(tc, x, weight_words, weight_scales, out):
                 out=w_codes[:].bitcast(I32),
                 in_=weight_words[0].rearrange("p n t -> p (n t)").bitcast(I32),
             )
-            for pair in range(2, PAIRS):
+            for pair in range(4, PAIRS):
                 load_x(pair)
 
-            stage_x(0)
-            stage_x(1)
-            quantise(0)
+            for pair in range(2):
+                stage_x(pair)
+            for pair in range(2):
+                quantise(pair)
             for group in range(GROUPS):
                 pairs = range(group * GROUP_PAIRS, (group + 1) * GROUP_PAIRS)
                 for pair in pairs:
-                    if pair + 2 < PAIRS:
-                        stage_x(pair + 2)
-                    if pair + 1 < PAIRS:
-                        quantise(pair + 1)
+                    for ahead in range(2 * pair + 2, min(2 * pair + 4, PAIRS)):
+                        stage_x(ahead)
+                    for ahead in range(max(2 * pair, 2), min(2 * pair + 2, PAIRS)):
+                        quantise(ahead)
                     tan_angles(pair)
                     tan_sine(pair)
                     if pair > pairs[0]:
                         tan_square(pair - 1)
                 tan_square(pairs[-1])
                 for pair in pairs:
-                    tan_secant(pair)
-                tiles = range(group * GROUP_TILES, (group + 1) * GROUP_TILES)
-                for t in tiles:
-                    due = t - LAG
-                    ys = [product(t, h) for h in range(HALVES)]
-                    count_turns(ys)
-                    if due >= tiles[0]:
-                        tan_product(due)
-                    take_turns_off(t, ys)
-                    sines(t)
-                    if due >= tiles[0]:
-                        interleave_and_store(due)
-                for due in tiles[-LAG:]:
-                    tan_product(due)
-                for due in tiles[-LAG:]:
-                    interleave_and_store(due)
+                    tan_finish(pair)
+                for t in range(pairs[0] * PAIR, (pairs[-1] + 1) * PAIR):
+                    main_angles(t)
+                    main_finish(t)

@@ -28,8 +28,12 @@ WORDS = K // 2
 
 PAIR = 2
 PAIRS = TILES // PAIR
+PAIR_BANKS = PAIR * HALVES
+PER_PAIR = PAIR * PER_TILE
 GROUPS = 2
 GROUP_PAIRS = PAIRS // GROUPS
+
+TAIL_TILES = 3
 
 TWO_PI = 2.0 * math.pi
 
@@ -54,10 +58,10 @@ def tile_mylayerfunc_kernel(tc, x, weight_words, weight_scales, out):
         x_scales = keep.tile([P, TILES * P], U8, align_bytes=64)
         w_codes = keep.tile([P, N], U32, align_bytes=64)
         w_scales = keep.tile([P, N], U8, align_bytes=64)
-        planes = keep.tile([P, TILES, CLASSES, PER_TILE], F32)
-        secant = keep.tile([P, TILES, PER_TILE], F32)
-        tan_turns = keep.tile([P, PAIR * HALVES, PER_BANK], I32)
-        turns = keep.tile([P, HALVES, TAN, PER_BANK], I32)
+        planes = keep.tile([P, PAIRS, CLASSES, PER_PAIR], F32)
+        secant = keep.tile([P, PAIRS, PER_PAIR], F32)
+        tan_turns = keep.tile([P, PAIR_BANKS, PER_BANK], I32)
+        turns = keep.tile([P, PAIR_BANKS, TAN, PER_BANK], I32)
         shifts = keep.tile([P, 2, 1], F32)
 
         def stage_x(pair):
@@ -94,9 +98,11 @@ def tile_mylayerfunc_kernel(tc, x, weight_words, weight_scales, out):
             return y[:].rearrange("p (c a) -> p a c", a=CLASSES)
 
 
+        def products(pair):
+            return [product(pair * PAIR + i, h) for i in range(PAIR) for h in range(HALVES)]
+
         def tan_angles(pair):
-            banks = [(pair * PAIR + i, h) for i in range(PAIR) for h in range(HALVES)]
-            ys = [product(t, h) for t, h in banks]
+            ys = products(pair)
             for b, y in enumerate(ys):
                 nc.vector.tensor_scalar(
                     out=tan_turns[:, b, :],
@@ -107,9 +113,8 @@ def tile_mylayerfunc_kernel(tc, x, weight_words, weight_scales, out):
                     op1=ALU.add,
                 )
             for b, y in enumerate(ys):
-                t, h = banks[b]
                 nc.vector.scalar_tensor_tensor(
-                    out=planes[:, t, TAN, h * PER_BANK : (h + 1) * PER_BANK],
+                    out=planes[:, pair, TAN, b * PER_BANK : (b + 1) * PER_BANK],
                     in0=tan_turns[:, b, :],
                     scalar=-math.pi,
                     in1=y[:, TAN, :],
@@ -118,58 +123,58 @@ def tile_mylayerfunc_kernel(tc, x, weight_words, weight_scales, out):
                 )
 
         def tan_sine(pair):
-            tiles = slice(pair * PAIR, (pair + 1) * PAIR)
-            nc.scalar.activation(out=planes[:, tiles, TAN, :], in_=planes[:, tiles, TAN, :], func=FUNC.Sin)
+            nc.scalar.activation(out=planes[:, pair, TAN, :], in_=planes[:, pair, TAN, :], func=FUNC.Sin)
 
         def tan_square(pair):
-            tiles = slice(pair * PAIR, (pair + 1) * PAIR)
-            nc.scalar.activation(out=secant[:, tiles, :], in_=planes[:, tiles, TAN, :], func=FUNC.Square)
+            nc.scalar.activation(out=secant[:, pair, :], in_=planes[:, pair, TAN, :], func=FUNC.Square)
 
         def tan_finish(pair):
-            tiles = slice(pair * PAIR, (pair + 1) * PAIR)
             nc.scalar.activation(
-                out=secant[:, tiles, :], in_=secant[:, tiles, :], func=FUNC.Abs_reciprocal_sqrt, bias=1.0, scale=-1.0
+                out=secant[:, pair, :], in_=secant[:, pair, :], func=FUNC.Abs_reciprocal_sqrt, bias=1.0, scale=-1.0
             )
             nc.gpsimd.tensor_tensor(
-                out=planes[:, tiles, TAN, :], in0=planes[:, tiles, TAN, :], in1=secant[:, tiles, :], op=ALU.mult
+                out=planes[:, pair, TAN, :], in0=planes[:, pair, TAN, :], in1=secant[:, pair, :], op=ALU.mult
             )
 
-        def main_angles(t):
-            ys = [product(t, h) for h in range(HALVES)]
-            for h, y in enumerate(ys):
+        def main_angles(pair):
+            ys = products(pair)
+            for b, y in enumerate(ys):
                 nc.vector.scalar_tensor_tensor(
-                    out=turns[:, h, COS:TAN, :],
+                    out=turns[:, b, COS:TAN, :],
                     in0=y[:, COS:TAN, :],
                     scalar=1.0 / TWO_PI,
                     in1=shifts[:].to_broadcast([P, 2, PER_BANK]),
                     op0=ALU.mult,
                     op1=ALU.add,
                 )
-            for h, y in enumerate(ys):
+            for b, y in enumerate(ys):
                 nc.vector.scalar_tensor_tensor(
-                    out=planes[:, t, LINEAR:TAN, h * PER_BANK : (h + 1) * PER_BANK],
-                    in0=turns[:, h, :, :],
+                    out=planes[:, pair, LINEAR:TAN, b * PER_BANK : (b + 1) * PER_BANK],
+                    in0=turns[:, b, :, :],
                     scalar=-TWO_PI,
                     in1=y[:, LINEAR:TAN, :],
                     op0=ALU.mult,
                     op1=ALU.add,
                 )
 
-        def main_finish(t):
+        def main_finish(pair):
             nc.scalar.activation(
-                out=planes[:, t, COS, :], in_=planes[:, t, COS, :], func=FUNC.Sin, bias=0.5 * math.pi
+                out=planes[:, pair, COS, :], in_=planes[:, pair, COS, :], func=FUNC.Sin, bias=0.5 * math.pi
             )
-            nc.scalar.activation(out=planes[:, t, SIN, :], in_=planes[:, t, SIN, :], func=FUNC.Sin)
-            result = work.tile([P, PER_TILE, CLASSES], F32)
-            nc.gpsimd.tensor_scalar(
-                out=result[:],
-                in0=planes[:, t, :, :].rearrange("p a j -> p j a"),
-                scalar1=1.0,
-                scalar2=0.0,
-                op0=ALU.mult,
-                op1=ALU.add,
-            )
-            nc.sync.dma_start(out=out_view[:, t, :], in_=result[:].rearrange("p j a -> p (j a)"))
+            nc.scalar.activation(out=planes[:, pair, SIN, :], in_=planes[:, pair, SIN, :], func=FUNC.Sin)
+            for i in range(PAIR):
+                t = pair * PAIR + i
+                by_column = planes[:, pair, :, i * PER_TILE : (i + 1) * PER_TILE].rearrange("p a j -> p j a")
+                if t < TILES - TAIL_TILES:
+                    result = work.tile([P, PER_TILE, CLASSES], F32)
+                    nc.gpsimd.tensor_scalar(
+                        out=result[:], in0=by_column, scalar1=1.0, scalar2=0.0, op0=ALU.mult, op1=ALU.add
+                    )
+                    nc.sync.dma_start(out=out_view[:, t, :], in_=result[:].rearrange("p j a -> p (j a)"))
+                else:
+                    result = work.tile([P, PER_TILE, CLASSES], F32, tag="tail_result")
+                    nc.scalar.copy(out=result[:], in_=by_column)
+                    nc.scalar.dma_start(out=out_view[:, t, :], in_=result[:].rearrange("p j a -> p (j a)"))
 
         def load_x(pair):
             tiles = slice(pair * PAIR, (pair + 1) * PAIR)
@@ -212,6 +217,6 @@ def tile_mylayerfunc_kernel(tc, x, weight_words, weight_scales, out):
                 tan_square(pairs[-1])
                 for pair in pairs:
                     tan_finish(pair)
-                for t in range(pairs[0] * PAIR, (pairs[-1] + 1) * PAIR):
-                    main_angles(t)
-                    main_finish(t)
+                for pair in pairs:
+                    main_angles(pair)
+                    main_finish(pair)

@@ -19,16 +19,13 @@ FLOPS = 2 * ROWS * K * N
 
 TILES = ROWS // P
 BANK = 512
-HALVES = N // BANK
 CLASSES = 4
 LINEAR, COS, SIN, TAN = 0, 1, 2, 3
-PER_BANK = BANK // CLASSES
 PER_TILE = N // CLASSES
 WORDS = K // 2
 
 PAIR = 2
 PAIRS = TILES // PAIR
-PAIR_BANKS = PAIR * HALVES
 PER_PAIR = PAIR * PER_TILE
 GROUPS = 2
 GROUP_PAIRS = PAIRS // GROUPS
@@ -56,12 +53,14 @@ def tile_mylayerfunc_kernel(tc, x, weight_words, weight_scales, out):
         grouped = keep.tile([P, TILES, P, 2], F32, align_bytes=64)
         x_codes = keep.tile([P, TILES * P], U32, align_bytes=64)
         x_scales = keep.tile([P, TILES * P], U8, align_bytes=64)
+        w_codes_in = keep.tile([P, N], U32)
+        w_scales_in = keep.tile([P, N], U8)
         w_codes = keep.tile([P, N], U32, align_bytes=64)
         w_scales = keep.tile([P, N], U8, align_bytes=64)
         planes = keep.tile([P, PAIRS, CLASSES, PER_PAIR], F32)
         secant = keep.tile([P, PAIRS, PER_PAIR], F32)
-        tan_turns = keep.tile([P, PAIR_BANKS, PER_BANK], I32)
-        turns = keep.tile([P, PAIR_BANKS, TAN, PER_BANK], I32)
+        tan_turns = keep.tile([P, 2, PER_PAIR], I32)
+        turns = keep.tile([P, PAIR, 2, PER_TILE], I32)
         shifts = keep.tile([P, 2, 1], F32)
 
         def stage_x(pair):
@@ -84,40 +83,42 @@ def tile_mylayerfunc_kernel(tc, x, weight_words, weight_scales, out):
                 in_=grouped[:, tiles, :, :].rearrange("p t r u -> p (t r u)").bitcast(BF16),
             )
 
-        def product(t, h):
-            y = psum_y.tile([P, BANK], F32)
+        def product(y, t, first, last):
+            cols = slice(first * PER_TILE, (last + 1) * PER_TILE)
             nc.tensor.matmul_mx(
-                out=y[:],
+                out=y,
                 lhsT=x_codes[:, t * P : (t + 1) * P].bitcast(FP8X4),
                 lhsT_scale=x_scales[:, t * P : (t + 1) * P],
-                rhs=w_codes[:, h * BANK : (h + 1) * BANK].bitcast(FP8X4),
-                rhs_scale=w_scales[:, h * BANK : (h + 1) * BANK],
+                rhs=w_codes[:, cols].bitcast(FP8X4),
+                rhs_scale=w_scales[:, cols],
                 start=True,
                 stop=True,
             )
-            return y[:].rearrange("p (c a) -> p a c", a=CLASSES)
+
+        def one_class(pair, a):
+            y = psum_y.tile([P, BANK], F32, tag="y")
+            for i in range(PAIR):
+                product(y[:, i * PER_TILE : (i + 1) * PER_TILE], pair * PAIR + i, a, a)
+            return y
+
+        def cos_and_sin(t):
+            y = psum_y.tile([P, BANK], F32, tag="y")
+            product(y[:], t, COS, SIN)
+            return y
 
 
-        def products(pair):
-            return [product(pair * PAIR + i, h) for i in range(PAIR) for h in range(HALVES)]
-
-        def tan_angles(pair):
-            ys = products(pair)
-            for b, y in enumerate(ys):
+        def tan_angles(two_pairs):
+            ys = [one_class(pair, TAN) for pair in two_pairs]
+            for s, y in enumerate(ys):
                 nc.vector.tensor_scalar(
-                    out=tan_turns[:, b, :],
-                    in0=y[:, TAN, :],
-                    scalar1=1.0 / math.pi,
-                    scalar2=0.0,
-                    op0=ALU.mult,
-                    op1=ALU.add,
+                    out=tan_turns[:, s, :], in0=y[:], scalar1=1.0 / math.pi, scalar2=0.0, op0=ALU.mult, op1=ALU.add
                 )
-            for b, y in enumerate(ys):
+            for s, y in enumerate(ys):
                 nc.vector.scalar_tensor_tensor(
-                    out=planes[:, pair, TAN, b * PER_BANK : (b + 1) * PER_BANK],
-                    in0=tan_turns[:, b, :],
+                    out=planes[:, two_pairs[s], TAN, :],
+                    in0=tan_turns[:, s, :],
                     scalar=-math.pi,
-                    in1=y[:, TAN, :],
+                    in1=y[:],
                     op0=ALU.mult,
                     op1=ALU.add,
                 )
@@ -137,22 +138,24 @@ def tile_mylayerfunc_kernel(tc, x, weight_words, weight_scales, out):
             )
 
         def main_angles(pair):
-            ys = products(pair)
-            for b, y in enumerate(ys):
+            ys = [cos_and_sin(pair * PAIR + i) for i in range(PAIR)]
+            linear = one_class(pair, LINEAR)
+            for i, y in enumerate(ys):
                 nc.vector.scalar_tensor_tensor(
-                    out=turns[:, b, COS:TAN, :],
-                    in0=y[:, COS:TAN, :],
+                    out=turns[:, i, :, :],
+                    in0=y[:].rearrange("p (a c) -> p a c", a=2),
                     scalar=1.0 / TWO_PI,
-                    in1=shifts[:].to_broadcast([P, 2, PER_BANK]),
+                    in1=shifts[:].to_broadcast([P, 2, PER_TILE]),
                     op0=ALU.mult,
                     op1=ALU.add,
                 )
-            for b, y in enumerate(ys):
+            nc.vector.tensor_copy(out=planes[:, pair, LINEAR, :], in_=linear[:])
+            for i, y in enumerate(ys):
                 nc.vector.scalar_tensor_tensor(
-                    out=planes[:, pair, LINEAR:TAN, b * PER_BANK : (b + 1) * PER_BANK],
-                    in0=turns[:, b, :, :],
+                    out=planes[:, pair, COS:TAN, i * PER_TILE : (i + 1) * PER_TILE],
+                    in0=turns[:, i, :, :],
                     scalar=-TWO_PI,
-                    in1=y[:, LINEAR:TAN, :],
+                    in1=y[:].rearrange("p (a c) -> p a c", a=2),
                     op0=ALU.mult,
                     op1=ALU.add,
                 )
@@ -181,23 +184,28 @@ def tile_mylayerfunc_kernel(tc, x, weight_words, weight_scales, out):
             nc.sync.dma_start(out=x_sb[:, tiles, :], in_=x_view[:, tiles, :])
 
         with tc.manual_schedule():
-            nc.vector.memset(w_scales[:].bitcast(I32), 0)
-            nc.vector.memset(turns[:, :, LINEAR, :], 0)
+            nc.vector.memset(w_scales_in[:].bitcast(I32), 0)
             nc.vector.memset(shifts[:, 0, :], 0.25)
             nc.vector.memset(shifts[:, 1, :], 0.0)
-            for pair in range(4):
-                load_x(pair)
             for quadrant in range(4):
                 nc.sync.dma_start(
-                    out=w_scales[32 * quadrant : 32 * quadrant + 4, :].bitcast(I32),
+                    out=w_scales_in[32 * quadrant : 32 * quadrant + 4, :].bitcast(I32),
                     in_=weight_scales[0, 4 * quadrant : 4 * quadrant + 4, :].bitcast(I32),
                 )
+            load_x(0)
             nc.sync.dma_start(
-                out=w_codes[:].bitcast(I32),
+                out=w_codes_in[:].bitcast(I32),
                 in_=weight_words[0].rearrange("p n t -> p (n t)").bitcast(I32),
             )
-            for pair in range(4, PAIRS):
+            for pair in range(1, PAIRS):
                 load_x(pair)
+
+            for a in range(CLASSES):
+                nc.vector.tensor_copy(out=w_scales[:, a * PER_TILE : (a + 1) * PER_TILE], in_=w_scales_in[:, a:N:CLASSES])
+            nc.vector.tensor_copy(
+                out=w_codes[:].bitcast(I32).rearrange("p (a c) -> p a c", a=CLASSES),
+                in_=w_codes_in[:].bitcast(I32).rearrange("p (c a) -> p a c", a=CLASSES),
+            )
 
             for pair in range(2):
                 stage_x(pair)
@@ -205,16 +213,17 @@ def tile_mylayerfunc_kernel(tc, x, weight_words, weight_scales, out):
                 quantise(pair)
             for group in range(GROUPS):
                 pairs = range(group * GROUP_PAIRS, (group + 1) * GROUP_PAIRS)
-                for pair in pairs:
-                    for ahead in range(2 * pair + 2, min(2 * pair + 4, PAIRS)):
+                for first in pairs[::2]:
+                    two_pairs = [first, first + 1]
+                    tan_angles(two_pairs)
+                    for ahead in range(2 * first + 2, min(2 * first + 6, PAIRS)):
                         stage_x(ahead)
-                    for ahead in range(max(2 * pair, 2), min(2 * pair + 2, PAIRS)):
+                    for pair in two_pairs:
+                        tan_sine(pair)
+                    for pair in two_pairs:
+                        tan_square(pair)
+                    for ahead in range(2 * first + 2, min(2 * first + 6, PAIRS)):
                         quantise(ahead)
-                    tan_angles(pair)
-                    tan_sine(pair)
-                    if pair > pairs[0]:
-                        tan_square(pair - 1)
-                tan_square(pairs[-1])
                 for pair in pairs:
                     tan_finish(pair)
                 for pair in pairs:

@@ -27,10 +27,11 @@ WORDS = K // 2
 PAIR = 2
 PAIRS = TILES // PAIR
 PER_PAIR = PAIR * PER_TILE
-GROUPS = 2
-GROUP_PAIRS = PAIRS // GROUPS
 
-TAIL_TILES = 3
+SCALAR_TILES = (1, 3, 5, 7, 9, 11)
+VECTOR_TILES = (13, 14, 15)
+SQUARES_ON_SCALAR = 4
+PRODUCTS_AHEAD = 6
 
 TWO_PI = 2.0 * math.pi
 
@@ -62,6 +63,7 @@ def tile_mylayerfunc_kernel(tc, x, weight_words, weight_scales, out):
         tan_turns = keep.tile([P, 2, PER_PAIR], I32)
         turns = keep.tile([P, PAIR, 2, PER_TILE], I32)
         shifts = keep.tile([P, 2, 1], F32)
+        warm = keep.tile([P, 1], F32)
 
         def stage_x(pair):
             xt = psum_x.tile([P, PAIR, 2, P], F32)
@@ -127,12 +129,19 @@ def tile_mylayerfunc_kernel(tc, x, weight_words, weight_scales, out):
             nc.scalar.activation(out=planes[:, pair, TAN, :], in_=planes[:, pair, TAN, :], func=FUNC.Sin)
 
         def tan_square(pair):
-            nc.scalar.activation(out=secant[:, pair, :], in_=planes[:, pair, TAN, :], func=FUNC.Square)
+            if pair < SQUARES_ON_SCALAR:
+                nc.scalar.activation(out=secant[:, pair, :], in_=planes[:, pair, TAN, :], func=FUNC.Square)
+            else:
+                nc.gpsimd.tensor_tensor(
+                    out=secant[:, pair, :], in0=planes[:, pair, TAN, :], in1=planes[:, pair, TAN, :], op=ALU.mult
+                )
 
-        def tan_finish(pair):
+        def tan_secant(pair):
             nc.scalar.activation(
                 out=secant[:, pair, :], in_=secant[:, pair, :], func=FUNC.Abs_reciprocal_sqrt, bias=1.0, scale=-1.0
             )
+
+        def tan_product(pair):
             nc.gpsimd.tensor_tensor(
                 out=planes[:, pair, TAN, :], in0=planes[:, pair, TAN, :], in1=secant[:, pair, :], op=ALU.mult
             )
@@ -160,72 +169,90 @@ def tile_mylayerfunc_kernel(tc, x, weight_words, weight_scales, out):
                     op1=ALU.add,
                 )
 
-        def main_finish(pair):
+        def main_sines(pair):
             nc.scalar.activation(
                 out=planes[:, pair, COS, :], in_=planes[:, pair, COS, :], func=FUNC.Sin, bias=0.5 * math.pi
             )
             nc.scalar.activation(out=planes[:, pair, SIN, :], in_=planes[:, pair, SIN, :], func=FUNC.Sin)
-            for i in range(PAIR):
-                t = pair * PAIR + i
-                by_column = planes[:, pair, :, i * PER_TILE : (i + 1) * PER_TILE].rearrange("p a j -> p j a")
-                if t < TILES - TAIL_TILES:
-                    result = work.tile([P, PER_TILE, CLASSES], F32)
-                    nc.gpsimd.tensor_scalar(
-                        out=result[:], in0=by_column, scalar1=1.0, scalar2=0.0, op0=ALU.mult, op1=ALU.add
-                    )
-                    nc.sync.dma_start(out=out_view[:, t, :], in_=result[:].rearrange("p j a -> p (j a)"))
-                else:
-                    result = work.tile([P, PER_TILE, CLASSES], F32, tag="tail_result")
-                    nc.scalar.copy(out=result[:], in_=by_column)
-                    nc.scalar.dma_start(out=out_view[:, t, :], in_=result[:].rearrange("p j a -> p (j a)"))
+
+        def finish(t):
+            pair, i = divmod(t, PAIR)
+            by_column = planes[:, pair, :, i * PER_TILE : (i + 1) * PER_TILE].rearrange("p a j -> p j a")
+            if t in SCALAR_TILES:
+                result = work.tile([P, PER_TILE, CLASSES], F32, tag="scalar_result")
+                nc.scalar.copy(out=result[:], in_=by_column)
+                nc.sync.dma_start(out=out_view[:, t, :], in_=result[:].rearrange("p j a -> p (j a)"))
+            elif t in VECTOR_TILES:
+                result = work.tile([P, PER_TILE, CLASSES], F32, tag="vector_result")
+                nc.vector.tensor_copy(out=result[:], in_=by_column)
+                nc.sync.dma_start(out=out_view[:, t, :], in_=result[:].rearrange("p j a -> p (j a)"))
+            else:
+                result = work.tile([P, PER_TILE, CLASSES], F32, tag="gpsimd_result")
+                nc.gpsimd.tensor_scalar(
+                    out=result[:], in0=by_column, scalar1=1.0, scalar2=0.0, op0=ALU.mult, op1=ALU.add
+                )
+                nc.sync.dma_start(out=out_view[:, t, :], in_=result[:].rearrange("p j a -> p (j a)"))
 
         def load_x(pair):
             tiles = slice(pair * PAIR, (pair + 1) * PAIR)
             nc.sync.dma_start(out=x_sb[:, tiles, :], in_=x_view[:, tiles, :])
 
+        def sort_w(classes):
+            for a in classes:
+                nc.vector.tensor_copy(out=w_scales[:, a * PER_TILE : (a + 1) * PER_TILE], in_=w_scales_in[:, a:N:CLASSES])
+            first, last = classes[0], classes[-1] + 1
+            nc.vector.tensor_copy(
+                out=w_codes[:, first * PER_TILE : last * PER_TILE].bitcast(I32).rearrange("p (a c) -> p a c", a=last - first),
+                in_=w_codes_in[:].bitcast(I32).rearrange("p (c a) -> p a c", a=CLASSES)[:, first:last, :],
+            )
+
         with tc.manual_schedule():
             nc.vector.memset(w_scales_in[:].bitcast(I32), 0)
             nc.vector.memset(shifts[:, 0, :], 0.25)
             nc.vector.memset(shifts[:, 1, :], 0.0)
-            for quadrant in range(4):
-                nc.sync.dma_start(
-                    out=w_scales_in[32 * quadrant : 32 * quadrant + 4, :].bitcast(I32),
-                    in_=weight_scales[0, 4 * quadrant : 4 * quadrant + 4, :].bitcast(I32),
-                )
+            nc.scalar.activation(out=warm[:], in_=shifts[:, 1, :], func=FUNC.Sin)
             load_x(0)
             nc.sync.dma_start(
                 out=w_codes_in[:].bitcast(I32),
                 in_=weight_words[0].rearrange("p n t -> p (n t)").bitcast(I32),
             )
+            for quadrant in range(4):
+                nc.sync.dma_start(
+                    out=w_scales_in[32 * quadrant : 32 * quadrant + 4, :].bitcast(I32),
+                    in_=weight_scales[0, 4 * quadrant : 4 * quadrant + 4, :].bitcast(I32),
+                )
             for pair in range(1, PAIRS):
                 load_x(pair)
 
-            for a in range(CLASSES):
-                nc.vector.tensor_copy(out=w_scales[:, a * PER_TILE : (a + 1) * PER_TILE], in_=w_scales_in[:, a:N:CLASSES])
-            nc.vector.tensor_copy(
-                out=w_codes[:].bitcast(I32).rearrange("p (a c) -> p a c", a=CLASSES),
-                in_=w_codes_in[:].bitcast(I32).rearrange("p (c a) -> p a c", a=CLASSES),
-            )
-
+            sort_w([TAN])
             for pair in range(2):
                 stage_x(pair)
             for pair in range(2):
                 quantise(pair)
-            for group in range(GROUPS):
-                pairs = range(group * GROUP_PAIRS, (group + 1) * GROUP_PAIRS)
-                for first in pairs[::2]:
-                    two_pairs = [first, first + 1]
-                    tan_angles(two_pairs)
-                    for ahead in range(2 * first + 2, min(2 * first + 6, PAIRS)):
-                        stage_x(ahead)
-                    for pair in two_pairs:
-                        tan_sine(pair)
-                    for pair in two_pairs:
-                        tan_square(pair)
-                    for ahead in range(2 * first + 2, min(2 * first + 6, PAIRS)):
-                        quantise(ahead)
-                for pair in pairs:
-                    tan_finish(pair)
-                for pair in pairs:
-                    main_angles(pair)
-                    main_finish(pair)
+            for first in range(0, PAIRS, 2):
+                two_pairs = [first, first + 1]
+                ahead = [pair for pair in (first + 2, first + 3) if pair < PAIRS]
+                tan_angles(two_pairs)
+                for pair in ahead:
+                    stage_x(pair)
+                for pair in two_pairs:
+                    tan_sine(pair)
+                for pair in two_pairs:
+                    tan_square(pair)
+                for pair in ahead:
+                    quantise(pair)
+            sort_w([LINEAR, COS, SIN])
+            for pair in range(PAIRS):
+                tan_secant(pair)
+            for pair in range(PRODUCTS_AHEAD):
+                tan_product(pair)
+            for pair in range(PAIRS):
+                main_angles(pair)
+                main_sines(pair)
+                for t in (pair * PAIR + 1, pair * PAIR):
+                    if t not in VECTOR_TILES:
+                        finish(t)
+                if pair + PRODUCTS_AHEAD < PAIRS:
+                    tan_product(pair + PRODUCTS_AHEAD)
+            for t in VECTOR_TILES:
+                finish(t)

@@ -29,7 +29,7 @@ PAIRS = TILES // PAIR
 PER_PAIR = PAIR * PER_TILE
 
 SCALAR_TILES = (1, 3, 5, 7, 9, 11)
-VECTOR_TILES = (13, 14, 15)
+VECTOR_TILES = (12, 13, 14, 15)
 SQUARES_ON_SCALAR = 4
 PRODUCTS_AHEAD = 6
 

@@ -109,12 +109,13 @@ def tile_mylayerfunc_kernel(tc, x, weight_words, weight_scales, out):
             return y
 
 
-        def tan_angles(two_pairs):
-            ys = [one_class(pair, TAN) for pair in two_pairs]
+        def tan_count(ys):
             for s, y in enumerate(ys):
                 nc.vector.tensor_scalar(
                     out=tan_turns[:, s, :], in0=y[:], scalar1=1.0 / math.pi, scalar2=0.0, op0=ALU.mult, op1=ALU.add
                 )
+
+        def tan_angles(two_pairs, ys):
             for s, y in enumerate(ys):
                 nc.vector.scalar_tensor_tensor(
                     out=planes[:, two_pairs[s], TAN, :],
@@ -211,7 +212,6 @@ def tile_mylayerfunc_kernel(tc, x, weight_words, weight_scales, out):
             nc.vector.memset(shifts[:, 0, :], 0.25)
             nc.vector.memset(shifts[:, 1, :], 0.0)
             nc.scalar.activation(out=warm[:], in_=shifts[:, 1, :], func=FUNC.Sin)
-            load_x(0)
             nc.sync.dma_start(
                 out=w_codes_in[:].bitcast(I32),
                 in_=weight_words[0].rearrange("p n t -> p (n t)").bitcast(I32),
@@ -221,27 +221,28 @@ def tile_mylayerfunc_kernel(tc, x, weight_words, weight_scales, out):
                     out=w_scales_in[32 * quadrant : 32 * quadrant + 4, :].bitcast(I32),
                     in_=weight_scales[0, 4 * quadrant : 4 * quadrant + 4, :].bitcast(I32),
                 )
-            for pair in range(1, PAIRS):
+            for pair in range(PAIRS):
                 load_x(pair)
 
             sort_w([TAN])
+            sort_w([LINEAR, COS, SIN])
             for pair in range(2):
                 stage_x(pair)
             for pair in range(2):
                 quantise(pair)
             for first in range(0, PAIRS, 2):
                 two_pairs = [first, first + 1]
-                ahead = [pair for pair in (first + 2, first + 3) if pair < PAIRS]
-                tan_angles(two_pairs)
-                for pair in ahead:
+                ys = [one_class(pair, TAN) for pair in two_pairs]
+                for pair in range(2 if first == 0 else first + 4, min(first + 6, PAIRS)):
                     stage_x(pair)
+                tan_count(ys)
+                for pair in range(first + 2, min(first + 4, PAIRS)):
+                    quantise(pair)
+                tan_angles(two_pairs, ys)
                 for pair in two_pairs:
                     tan_sine(pair)
                 for pair in two_pairs:
                     tan_square(pair)
-                for pair in ahead:
-                    quantise(pair)
-            sort_w([LINEAR, COS, SIN])
             for pair in range(PAIRS):
                 tan_secant(pair)
             for pair in range(PRODUCTS_AHEAD):

@@ -28,8 +28,8 @@ PAIR = 2
 PAIRS = TILES // PAIR
 PER_PAIR = PAIR * PER_TILE
 
-SCALAR_TILES = (1, 3, 5, 7, 9, 11)
-VECTOR_TILES = (12, 13, 14, 15)
+SCALAR_TILES = (1, 3, 5, 7, 9)
+VECTOR_TILES = (10, 11, 12, 13, 14, 15)
 SQUARES_ON_SCALAR = 4
 PRODUCTS_AHEAD = 6
 

@@ -31,7 +31,7 @@ PER_PAIR = PAIR * PER_TILE
 SCALAR_TILES = (1, 3, 5, 7, 9)
 VECTOR_TILES = (10, 11, 12, 13, 14, 15)
 SQUARES_ON_SCALAR = 4
-PRODUCTS_AHEAD = 6
+PRODUCTS_AHEAD = 5
 
 TWO_PI = 2.0 * math.pi
 

@@ -22,6 +22,7 @@ BANK = 512
 CLASSES = 4
 LINEAR, COS, SIN, TAN = 0, 1, 2, 3
 PER_TILE = N // CLASSES
+LINE = 4
 WORDS = K // 2
 
 PAIR = 2
@@ -178,21 +179,17 @@ def tile_mylayerfunc_kernel(tc, x, weight_words, weight_scales, out):
 
         def finish(t):
             pair, i = divmod(t, PAIR)
-            by_column = planes[:, pair, :, i * PER_TILE : (i + 1) * PER_TILE].rearrange("p a j -> p j a")
-            if t in SCALAR_TILES:
-                result = work.tile([P, PER_TILE, CLASSES], F32, tag="scalar_result")
-                nc.scalar.copy(out=result[:], in_=by_column)
-                nc.sync.dma_start(out=out_view[:, t, :], in_=result[:].rearrange("p j a -> p (j a)"))
-            elif t in VECTOR_TILES:
-                result = work.tile([P, PER_TILE, CLASSES], F32, tag="vector_result")
-                nc.vector.tensor_copy(out=result[:], in_=by_column)
-                nc.sync.dma_start(out=out_view[:, t, :], in_=result[:].rearrange("p j a -> p (j a)"))
+            source = planes[:, pair, :, i * PER_TILE : (i + 1) * PER_TILE].rearrange("p a (c e) -> p c a e", e=LINE)
+            engine = "scalar" if t in SCALAR_TILES else "vector" if t in VECTOR_TILES else "gpsimd"
+            result = work.tile([P, PER_TILE, CLASSES], F32, tag=engine + "_result")
+            target = result[:].rearrange("p (c e) a -> p c a e", e=LINE)
+            if engine == "scalar":
+                nc.scalar.copy(out=target, in_=source)
+            elif engine == "vector":
+                nc.vector.tensor_copy(out=target, in_=source)
             else:
-                result = work.tile([P, PER_TILE, CLASSES], F32, tag="gpsimd_result")
-                nc.gpsimd.tensor_scalar(
-                    out=result[:], in0=by_column, scalar1=1.0, scalar2=0.0, op0=ALU.mult, op1=ALU.add
-                )
-                nc.sync.dma_start(out=out_view[:, t, :], in_=result[:].rearrange("p j a -> p (j a)"))
+                nc.gpsimd.tensor_scalar(out=target, in0=source, scalar1=1.0, scalar2=0.0, op0=ALU.mult, op1=ALU.add)
+            nc.sync.dma_start(out=out_view[:, t, :], in_=result[:].rearrange("p j a -> p (j a)"))
 
         def load_x(pair):
             tiles = slice(pair * PAIR, (pair + 1) * PAIR)

@@ -34,6 +34,8 @@ VECTOR_TILES = (10, 11, 12, 13, 14, 15)
 SQUARES_ON_SCALAR = 4
 PRODUCTS_AHEAD = 5
 
+FIRST_FILLERS = 5
+
 TWO_PI = 2.0 * math.pi
 
 
@@ -68,6 +70,8 @@ def tile_mylayerfunc_kernel(tc, x, weight_words, weight_scales, out):
 
         def stage_x(pair):
             xt = psum_x.tile([P, PAIR, 2, P], F32)
+            for filler in range(FIRST_FILLERS if pair == 0 else 1):
+                nc.tensor.matmul(xt[:, 0, 0, :], ident[:], ident[:], start=True, stop=True)
             for i in range(PAIR):
                 words = x_sb[:, pair * PAIR + i, :].bitcast(F32)
                 for u in range(2):

@@ -31,10 +31,8 @@ PER_PAIR = PAIR * PER_TILE
 
 SCALAR_TILES = (1, 3, 5, 7, 9)
 VECTOR_TILES = (10, 11, 12, 13, 14, 15)
-SQUARES_ON_SCALAR = 4
+SQUARES_ON_SCALAR = (0, 1)
 PRODUCTS_AHEAD = 5
-
-FIRST_FILLERS = 5
 
 TWO_PI = 2.0 * math.pi
 
@@ -63,15 +61,13 @@ def tile_mylayerfunc_kernel(tc, x, weight_words, weight_scales, out):
         w_scales = keep.tile([P, N], U8, align_bytes=64)
         planes = keep.tile([P, PAIRS, CLASSES, PER_PAIR], F32)
         secant = keep.tile([P, PAIRS, PER_PAIR], F32)
-        tan_turns = keep.tile([P, 2, PER_PAIR], I32)
+        tan_turns = keep.tile([P, 4, PER_PAIR], I32)
         turns = keep.tile([P, PAIR, 2, PER_TILE], I32)
         shifts = keep.tile([P, 2, 1], F32)
         warm = keep.tile([P, 1], F32)
 
         def stage_x(pair):
             xt = psum_x.tile([P, PAIR, 2, P], F32)
-            for filler in range(FIRST_FILLERS if pair == 0 else 1):
-                nc.tensor.matmul(xt[:, 0, 0, :], ident[:], ident[:], start=True, stop=True)
             for i in range(PAIR):
                 words = x_sb[:, pair * PAIR + i, :].bitcast(F32)
                 for u in range(2):
@@ -114,28 +110,31 @@ def tile_mylayerfunc_kernel(tc, x, weight_words, weight_scales, out):
             return y
 
 
-        def tan_count(ys):
-            for s, y in enumerate(ys):
+        def tan_count(pair, y):
+            if pair % 2 == 0:
                 nc.vector.tensor_scalar(
-                    out=tan_turns[:, s, :], in0=y[:], scalar1=1.0 / math.pi, scalar2=0.0, op0=ALU.mult, op1=ALU.add
+                    out=tan_turns[:, pair % 4, :], in0=y[:], scalar1=1.0 / math.pi, scalar2=0.0, op0=ALU.mult, op1=ALU.add
+                )
+            else:
+                nc.scalar.activation(
+                    out=tan_turns[:, pair % 4, :].bitcast(U32), in_=y[:], func=FUNC.Copy, scale=1.0 / math.pi
                 )
 
-        def tan_angles(two_pairs, ys):
-            for s, y in enumerate(ys):
-                nc.vector.scalar_tensor_tensor(
-                    out=planes[:, two_pairs[s], TAN, :],
-                    in0=tan_turns[:, s, :],
-                    scalar=-math.pi,
-                    in1=y[:],
-                    op0=ALU.mult,
-                    op1=ALU.add,
-                )
+        def tan_angle(pair, y):
+            nc.vector.scalar_tensor_tensor(
+                out=planes[:, pair, TAN, :],
+                in0=tan_turns[:, pair % 4, :],
+                scalar=-math.pi,
+                in1=y[:],
+                op0=ALU.mult,
+                op1=ALU.add,
+            )
 
         def tan_sine(pair):
             nc.scalar.activation(out=planes[:, pair, TAN, :], in_=planes[:, pair, TAN, :], func=FUNC.Sin)
 
         def tan_square(pair):
-            if pair < SQUARES_ON_SCALAR:
+            if pair in SQUARES_ON_SCALAR:
                 nc.scalar.activation(out=secant[:, pair, :], in_=planes[:, pair, TAN, :], func=FUNC.Square)
             else:
                 nc.gpsimd.tensor_tensor(
@@ -183,16 +182,19 @@ def tile_mylayerfunc_kernel(tc, x, weight_words, weight_scales, out):
 
         def finish(t):
             pair, i = divmod(t, PAIR)
-            source = planes[:, pair, :, i * PER_TILE : (i + 1) * PER_TILE].rearrange("p a (c e) -> p c a e", e=LINE)
+            by_class = planes[:, pair, :, i * PER_TILE : (i + 1) * PER_TILE]
             engine = "scalar" if t in SCALAR_TILES else "vector" if t in VECTOR_TILES else "gpsimd"
             result = work.tile([P, PER_TILE, CLASSES], F32, tag=engine + "_result")
-            target = result[:].rearrange("p (c e) a -> p c a e", e=LINE)
+            blocks_in = by_class.rearrange("p a (c e) -> p c a e", e=LINE)
+            blocks_out = result[:].rearrange("p (c e) a -> p c a e", e=LINE)
             if engine == "scalar":
-                nc.scalar.copy(out=target, in_=source)
+                nc.scalar.copy(out=blocks_out, in_=blocks_in)
             elif engine == "vector":
-                nc.vector.tensor_copy(out=target, in_=source)
+                nc.vector.tensor_copy(out=blocks_out, in_=blocks_in)
             else:
-                nc.gpsimd.tensor_scalar(out=target, in0=source, scalar1=1.0, scalar2=0.0, op0=ALU.mult, op1=ALU.add)
+                nc.gpsimd.tensor_scalar(
+                    out=result[:], in0=by_class.rearrange("p a j -> p j a"), scalar1=1.0, scalar2=0.0, op0=ALU.mult, op1=ALU.add
+                )
             nc.sync.dma_start(out=out_view[:, t, :], in_=result[:].rearrange("p j a -> p (j a)"))
 
         def load_x(pair):
@@ -227,23 +229,32 @@ def tile_mylayerfunc_kernel(tc, x, weight_words, weight_scales, out):
 
             sort_w([TAN])
             sort_w([LINEAR, COS, SIN])
-            for pair in range(2):
+            for pair in range(4):
                 stage_x(pair)
             for pair in range(2):
                 quantise(pair)
             for first in range(0, PAIRS, 2):
-                two_pairs = [first, first + 1]
-                ys = [one_class(pair, TAN) for pair in two_pairs]
-                for pair in range(2 if first == 0 else first + 4, min(first + 6, PAIRS)):
-                    stage_x(pair)
-                tan_count(ys)
+                now = (first, first + 1)
+                before = (first - 2, first - 1) if first else ()
+                ys = [one_class(pair, TAN) for pair in now]
+                for pair, y in zip(now, ys):
+                    tan_count(pair, y)
+                for pair in before:
+                    tan_sine(pair)
+                    if pair not in SQUARES_ON_SCALAR:
+                        tan_square(pair)
+                if first == 4:
+                    for pair in SQUARES_ON_SCALAR:
+                        tan_square(pair)
                 for pair in range(first + 2, min(first + 4, PAIRS)):
                     quantise(pair)
-                tan_angles(two_pairs, ys)
-                for pair in two_pairs:
-                    tan_sine(pair)
-                for pair in two_pairs:
-                    tan_square(pair)
+                for pair in range(first + 4, min(first + 6, PAIRS)):
+                    stage_x(pair)
+                for pair, y in zip(now, ys):
+                    tan_angle(pair, y)
+            for pair in now:
+                tan_sine(pair)
+                tan_square(pair)
             for pair in range(PAIRS):
                 tan_secant(pair)
             for pair in range(PRODUCTS_AHEAD):

@@ -30,8 +30,9 @@ PAIRS = TILES // PAIR
 PER_PAIR = PAIR * PER_TILE
 
 SCALAR_TILES = (1, 3, 5, 7, 9)
-VECTOR_TILES = (10, 11, 12, 13, 14, 15)
-SQUARES_ON_SCALAR = (0, 1)
+VECTOR_TILES = (0, 10, 11, 12, 13, 14, 15)
+LEAD = 3
+SQUARES_ON_SCALAR = (0,)
 PRODUCTS_AHEAD = 5
 
 TWO_PI = 2.0 * math.pi
@@ -174,11 +175,10 @@ def tile_mylayerfunc_kernel(tc, x, weight_words, weight_scales, out):
                     op1=ALU.add,
                 )
 
-        def main_sines(pair):
-            nc.scalar.activation(
-                out=planes[:, pair, COS, :], in_=planes[:, pair, COS, :], func=FUNC.Sin, bias=0.5 * math.pi
-            )
-            nc.scalar.activation(out=planes[:, pair, SIN, :], in_=planes[:, pair, SIN, :], func=FUNC.Sin)
+        def main_sines(pair, first, last):
+            cols = slice(first * PER_TILE, (last + 1) * PER_TILE)
+            for a, bias in ((COS, 0.5 * math.pi), (SIN, 0.0)):
+                nc.scalar.activation(out=planes[:, pair, a, cols], in_=planes[:, pair, a, cols], func=FUNC.Sin, bias=bias)
 
         def finish(t):
             pair, i = divmod(t, PAIR)
@@ -259,13 +259,20 @@ def tile_mylayerfunc_kernel(tc, x, weight_words, weight_scales, out):
                 tan_secant(pair)
             for pair in range(PRODUCTS_AHEAD):
                 tan_product(pair)
-            for pair in range(PAIRS):
+            for pair in range(LEAD):
                 main_angles(pair)
-                main_sines(pair)
-                for t in (pair * PAIR + 1, pair * PAIR):
-                    if t not in VECTOR_TILES:
-                        finish(t)
+            for pair in range(PAIRS):
+                if pair + LEAD < PAIRS:
+                    main_angles(pair + LEAD)
+                if pair > 0:
+                    main_sines(pair, 0, 1)
+                for i in (1, 0):
+                    if pair == 0:
+                        main_sines(pair, i, i)
+                    if pair * PAIR + i < VECTOR_TILES[1]:
+                        finish(pair * PAIR + i)
                 if pair + PRODUCTS_AHEAD < PAIRS:
                     tan_product(pair + PRODUCTS_AHEAD)
-            for t in VECTOR_TILES:
-                finish(t)
+                for t in VECTOR_TILES[1:]:
+                    if t // PAIR == pair:
+                        finish(t)

@@ -29,8 +29,9 @@ PAIR = 2
 PAIRS = TILES // PAIR
 PER_PAIR = PAIR * PER_TILE
 
-SCALAR_TILES = (1, 3, 5, 7, 9)
-VECTOR_TILES = (0, 10, 11, 12, 13, 14, 15)
+SCALAR_TILES = (3, 5, 7, 9)
+VECTOR_TILES = (0, 1, 10, 11, 12, 13, 14, 15)
+SCALAR_LINEAR = (6, 7)
 LEAD = 3
 SQUARES_ON_SCALAR = (0,)
 PRODUCTS_AHEAD = 5
@@ -152,9 +153,12 @@ def tile_mylayerfunc_kernel(tc, x, weight_words, weight_scales, out):
                 out=planes[:, pair, TAN, :], in0=planes[:, pair, TAN, :], in1=secant[:, pair, :], op=ALU.mult
             )
 
-        def main_angles(pair):
+        banks = {}
+
+        def main_turns(pair):
             ys = [cos_and_sin(pair * PAIR + i) for i in range(PAIR)]
             linear = one_class(pair, LINEAR)
+            banks[pair] = ys, linear
             for i, y in enumerate(ys):
                 nc.vector.scalar_tensor_tensor(
                     out=turns[:, i, :, :],
@@ -164,8 +168,11 @@ def tile_mylayerfunc_kernel(tc, x, weight_words, weight_scales, out):
                     op0=ALU.mult,
                     op1=ALU.add,
                 )
-            nc.vector.tensor_copy(out=planes[:, pair, LINEAR, :], in_=linear[:])
-            for i, y in enumerate(ys):
+            if pair not in SCALAR_LINEAR:
+                nc.vector.tensor_copy(out=planes[:, pair, LINEAR, :], in_=linear[:])
+
+        def main_angles(pair):
+            for i, y in enumerate(banks[pair][0]):
                 nc.vector.scalar_tensor_tensor(
                     out=planes[:, pair, COS:TAN, i * PER_TILE : (i + 1) * PER_TILE],
                     in0=turns[:, i, :, :],
@@ -260,19 +267,22 @@ def tile_mylayerfunc_kernel(tc, x, weight_words, weight_scales, out):
             for pair in range(PRODUCTS_AHEAD):
                 tan_product(pair)
             for pair in range(LEAD):
+                main_turns(pair)
                 main_angles(pair)
-            for pair in range(PAIRS):
+            main_turns(LEAD)
+            main_sines(0, 1, 1)
+            finish(1)
+            main_angles(LEAD)
+            main_sines(0, 0, 0)
+            finish(0)
+            for pair in range(1, PAIRS):
                 if pair + LEAD < PAIRS:
+                    main_turns(pair + LEAD)
                     main_angles(pair + LEAD)
-                if pair > 0:
-                    main_sines(pair, 0, 1)
-                for i in (1, 0):
-                    if pair == 0:
-                        main_sines(pair, i, i)
-                    if pair * PAIR + i < VECTOR_TILES[1]:
-                        finish(pair * PAIR + i)
-                if pair + PRODUCTS_AHEAD < PAIRS:
-                    tan_product(pair + PRODUCTS_AHEAD)
-                for t in VECTOR_TILES[1:]:
-                    if t // PAIR == pair:
-                        finish(t)
+                if pair + 1 in SCALAR_LINEAR:
+                    nc.scalar.copy(out=planes[:, pair + 1, LINEAR, :], in_=banks[pair + 1][1][:])
+                main_sines(pair, 0, 1)
+                for t in (pair * PAIR + 1, pair * PAIR) if pair < 5 else (pair * PAIR, pair * PAIR + 1):
+                    finish(t)
+                if pair + PRODUCTS_AHEAD - 1 < PAIRS:
+                    tan_product(pair + PRODUCTS_AHEAD - 1)

@@ -100,8 +100,9 @@ def tile_mylayerfunc_kernel(tc, x, weight_words, weight_scales, out):
                 stop=True,
             )
 
-        def one_class(pair, a):
-            y = psum_y.tile([P, BANK], F32, tag="y")
+        def one_class(pair, a, y=None):
+            if y is None:
+                y = psum_y.tile([P, BANK], F32, tag="y")
             for i in range(PAIR):
                 product(y[:, i * PER_TILE : (i + 1) * PER_TILE], pair * PAIR + i, a, a)
             return y
@@ -236,14 +237,23 @@ def tile_mylayerfunc_kernel(tc, x, weight_words, weight_scales, out):
 
             sort_w([TAN])
             sort_w([LINEAR, COS, SIN])
+            first_y = psum_y.tile([P, BANK], F32, tag="y")
+
+            def fill(count):
+                for n in range(count):
+                    nc.tensor.matmul(first_y[:, :P], ident[:], ident[:], start=True, stop=True)
+
+            fill(5)
             for pair in range(4):
+                if pair == 2:
+                    fill(1)
                 stage_x(pair)
             for pair in range(2):
                 quantise(pair)
             for first in range(0, PAIRS, 2):
                 now = (first, first + 1)
                 before = (first - 2, first - 1) if first else ()
-                ys = [one_class(pair, TAN) for pair in now]
+                ys = [one_class(pair, TAN, None if pair else first_y) for pair in now]
                 for pair, y in zip(now, ys):
                     tan_count(pair, y)
                 for pair in before:

import math
from contextlib import ExitStack

import concourse.mybir as mybir
from concourse.masks import make_identity

F32 = mybir.dt.float32
BF16 = mybir.dt.bfloat16
I32 = mybir.dt.int32
U32 = mybir.dt.uint32
U8 = mybir.dt.uint8
FP8X4 = mybir.dt.float8_e4m3fn_x4
FUNC = mybir.ActivationFunctionType
ALU = mybir.AluOpType

P = 128
ROWS, K, N = 2048, 512, 1024
FLOPS = 2 * ROWS * K * N

TILES = ROWS // P
BANK = 512
CLASSES = 4
LINEAR, COS, SIN, TAN = 0, 1, 2, 3
PER_TILE = N // CLASSES
LINE = 4
WORDS = K // 2

PAIR = 2
PAIRS = TILES // PAIR
PER_PAIR = PAIR * PER_TILE

SCALAR_TILES = (3, 5, 7, 9)
VECTOR_TILES = (0, 1, 10, 11, 12, 13, 14, 15)
SCALAR_LINEAR = (6, 7)
LEAD = 3
SQUARES_ON_SCALAR = (0,)
PRODUCTS_AHEAD = 5

TWO_PI = 2.0 * math.pi


def tile_mylayerfunc_kernel(tc, x, weight_words, weight_scales, out):
    nc = tc.nc
    with ExitStack() as ctx:
        keep = ctx.enter_context(tc.tile_pool(name="keep", bufs=1))
        work = ctx.enter_context(tc.tile_pool(name="work", bufs=4))
        psum_x = ctx.enter_context(tc.psum_pool(name="psum_x", bufs=2))
        psum_y = ctx.enter_context(tc.psum_pool(name="psum_y", bufs=6))

        x_view = x.rearrange("(p t) k -> p t k", t=TILES)
        out_view = out.rearrange("(p t) n -> p t n", t=TILES)

        ident = keep.tile([P, P], F32)
        make_identity(nc, ident[:])

        x_sb = keep.tile([P, TILES, K], BF16)
        grouped = keep.tile([P, TILES, P, 2], F32, align_bytes=64)
        x_codes = keep.tile([P, TILES * P], U32, align_bytes=64)
        x_scales = keep.tile([P, TILES * P], U8, align_bytes=64)
        w_codes_in = keep.tile([P, N], U32)
        w_scales_in = keep.tile([P, N], U8)
        w_codes = keep.tile([P, N], U32, align_bytes=64)
        w_scales = keep.tile([P, N], U8, align_bytes=64)
        planes = keep.tile([P, PAIRS, CLASSES, PER_PAIR], F32)
        secant = keep.tile([P, PAIRS, PER_PAIR], F32)
        tan_turns = keep.tile([P, 4, PER_PAIR], I32)
        turns = keep.tile([P, PAIR, 2, PER_TILE], I32)
        shifts = keep.tile([P, 2, 1], F32)
        warm = keep.tile([P, 1], F32)

        def stage_x(pair):
            xt = psum_x.tile([P, PAIR, 2, P], F32)
            for i in range(PAIR):
                words = x_sb[:, pair * PAIR + i, :].bitcast(F32)
                for u in range(2):
                    nc.tensor.transpose(xt[:, i, u, :], words[:, u:WORDS:2], ident[:])
            nc.scalar.copy(
                out=grouped[:, pair * PAIR : (pair + 1) * PAIR, :, :],
                in_=xt[:].rearrange("p i u r -> p i r u"),
            )

        def quantise(pair):
            tiles = slice(pair * PAIR, (pair + 1) * PAIR)
            cols = slice(pair * PAIR * P, (pair + 1) * PAIR * P)
            nc.vector.quantize_mx(
                out=x_codes[:, cols].bitcast(FP8X4),
                scales=x_scales[:, cols],
                in_=grouped[:, tiles, :, :].rearrange("p t r u -> p (t r u)").bitcast(BF16),
            )

        def product(y, t, first, last):
            cols = slice(first * PER_TILE, (last + 1) * PER_TILE)
            nc.tensor.matmul_mx(
                out=y,
                lhsT=x_codes[:, t * P : (t + 1) * P].bitcast(FP8X4),
                lhsT_scale=x_scales[:, t * P : (t + 1) * P],
                rhs=w_codes[:, cols].bitcast(FP8X4),
                rhs_scale=w_scales[:, cols],
                start=True,
                stop=True,
            )

        def one_class(pair, a, y=None):
            if y is None:
                y = psum_y.tile([P, BANK], F32, tag="y")
            for i in range(PAIR):
                product(y[:, i * PER_TILE : (i + 1) * PER_TILE], pair * PAIR + i, a, a)
            return y

        def cos_and_sin(t):
            y = psum_y.tile([P, BANK], F32, tag="y")
            product(y[:], t, COS, SIN)
            return y


        def tan_count(pair, y):
            if pair % 2 == 0:
                nc.vector.tensor_scalar(
                    out=tan_turns[:, pair % 4, :], in0=y[:], scalar1=1.0 / math.pi, scalar2=0.0, op0=ALU.mult, op1=ALU.add
                )
            else:
                nc.scalar.activation(
                    out=tan_turns[:, pair % 4, :].bitcast(U32), in_=y[:], func=FUNC.Copy, scale=1.0 / math.pi
                )

        def tan_angle(pair, y):
            nc.vector.scalar_tensor_tensor(
                out=planes[:, pair, TAN, :],
                in0=tan_turns[:, pair % 4, :],
                scalar=-math.pi,
                in1=y[:],
                op0=ALU.mult,
                op1=ALU.add,
            )

        def tan_sine(pair):
            nc.scalar.activation(out=planes[:, pair, TAN, :], in_=planes[:, pair, TAN, :], func=FUNC.Sin)

        def tan_square(pair):
            if pair in SQUARES_ON_SCALAR:
                nc.scalar.activation(out=secant[:, pair, :], in_=planes[:, pair, TAN, :], func=FUNC.Square)
            else:
                nc.gpsimd.tensor_tensor(
                    out=secant[:, pair, :], in0=planes[:, pair, TAN, :], in1=planes[:, pair, TAN, :], op=ALU.mult
                )

        def tan_secant(pair):
            nc.scalar.activation(
                out=secant[:, pair, :], in_=secant[:, pair, :], func=FUNC.Abs_reciprocal_sqrt, bias=1.0, scale=-1.0
            )

        def tan_product(pair):
            nc.gpsimd.tensor_tensor(
                out=planes[:, pair, TAN, :], in0=planes[:, pair, TAN, :], in1=secant[:, pair, :], op=ALU.mult
            )

        banks = {}

        def main_turns(pair):
            ys = [cos_and_sin(pair * PAIR + i) for i in range(PAIR)]
            linear = one_class(pair, LINEAR)
            banks[pair] = ys, linear
            for i, y in enumerate(ys):
                nc.vector.scalar_tensor_tensor(
                    out=turns[:, i, :, :],
                    in0=y[:].rearrange("p (a c) -> p a c", a=2),
                    scalar=1.0 / TWO_PI,
                    in1=shifts[:].to_broadcast([P, 2, PER_TILE]),
                    op0=ALU.mult,
                    op1=ALU.add,
                )
            if pair not in SCALAR_LINEAR:
                nc.vector.tensor_copy(out=planes[:, pair, LINEAR, :], in_=linear[:])

        def main_angles(pair):
            for i, y in enumerate(banks[pair][0]):
                nc.vector.scalar_tensor_tensor(
                    out=planes[:, pair, COS:TAN, i * PER_TILE : (i + 1) * PER_TILE],
                    in0=turns[:, i, :, :],
                    scalar=-TWO_PI,
                    in1=y[:].rearrange("p (a c) -> p a c", a=2),
                    op0=ALU.mult,
                    op1=ALU.add,
                )

        def main_sines(pair, first, last):
            cols = slice(first * PER_TILE, (last + 1) * PER_TILE)
            for a, bias in ((COS, 0.5 * math.pi), (SIN, 0.0)):
                nc.scalar.activation(out=planes[:, pair, a, cols], in_=planes[:, pair, a, cols], func=FUNC.Sin, bias=bias)

        def finish(t):
            pair, i = divmod(t, PAIR)
            by_class = planes[:, pair, :, i * PER_TILE : (i + 1) * PER_TILE]
            engine = "scalar" if t in SCALAR_TILES else "vector" if t in VECTOR_TILES else "gpsimd"
            result = work.tile([P, PER_TILE, CLASSES], F32, tag=engine + "_result")
            blocks_in = by_class.rearrange("p a (c e) -> p c a e", e=LINE)
            blocks_out = result[:].rearrange("p (c e) a -> p c a e", e=LINE)
            if engine == "scalar":
                nc.scalar.copy(out=blocks_out, in_=blocks_in)
            elif engine == "vector":
                nc.vector.tensor_copy(out=blocks_out, in_=blocks_in)
            else:
                nc.gpsimd.tensor_scalar(
                    out=result[:], in0=by_class.rearrange("p a j -> p j a"), scalar1=1.0, scalar2=0.0, op0=ALU.mult, op1=ALU.add
                )
            nc.sync.dma_start(out=out_view[:, t, :], in_=result[:].rearrange("p j a -> p (j a)"))

        def load_x(pair):
            tiles = slice(pair * PAIR, (pair + 1) * PAIR)
            nc.sync.dma_start(out=x_sb[:, tiles, :], in_=x_view[:, tiles, :])

        def sort_w(classes):
            for a in classes:
                nc.vector.tensor_copy(out=w_scales[:, a * PER_TILE : (a + 1) * PER_TILE], in_=w_scales_in[:, a:N:CLASSES])
            first, last = classes[0], classes[-1] + 1
            nc.vector.tensor_copy(
                out=w_codes[:, first * PER_TILE : last * PER_TILE].bitcast(I32).rearrange("p (a c) -> p a c", a=last - first),
                in_=w_codes_in[:].bitcast(I32).rearrange("p (c a) -> p a c", a=CLASSES)[:, first:last, :],
            )

        with tc.manual_schedule():
            nc.vector.memset(w_scales_in[:].bitcast(I32), 0)
            nc.vector.memset(shifts[:, 0, :], 0.25)
            nc.vector.memset(shifts[:, 1, :], 0.0)
            nc.scalar.activation(out=warm[:], in_=shifts[:, 1, :], func=FUNC.Sin)
            nc.sync.dma_start(
                out=w_codes_in[:].bitcast(I32),
                in_=weight_words[0].rearrange("p n t -> p (n t)").bitcast(I32),
            )
            for quadrant in range(4):
                nc.sync.dma_start(
                    out=w_scales_in[32 * quadrant : 32 * quadrant + 4, :].bitcast(I32),
                    in_=weight_scales[0, 4 * quadrant : 4 * quadrant + 4, :].bitcast(I32),
                )
            for pair in range(PAIRS):
                load_x(pair)

            sort_w([TAN])
            sort_w([LINEAR, COS, SIN])
            first_y = psum_y.tile([P, BANK], F32, tag="y")

            def fill(count):
                for n in range(count):
                    nc.tensor.matmul(first_y[:, :P], ident[:], ident[:], start=True, stop=True)

            fill(5)
            for pair in range(4):
                if pair == 2:
                    fill(1)
                stage_x(pair)
            for pair in range(2):
                quantise(pair)
            for first in range(0, PAIRS, 2):
                now = (first, first + 1)
                before = (first - 2, first - 1) if first else ()
                ys = [one_class(pair, TAN, None if pair else first_y) for pair in now]
                for pair, y in zip(now, ys):
                    tan_count(pair, y)
                for pair in before:
                    tan_sine(pair)
                    if pair not in SQUARES_ON_SCALAR:
                        tan_square(pair)
                if first == 4:
                    for pair in SQUARES_ON_SCALAR:
                        tan_square(pair)
                for pair in range(first + 2, min(first + 4, PAIRS)):
                    quantise(pair)
                for pair in range(first + 4, min(first + 6, PAIRS)):
                    stage_x(pair)
                for pair, y in zip(now, ys):
                    tan_angle(pair, y)
            for pair in now:
                tan_sine(pair)
                tan_square(pair)
            for pair in range(PAIRS):
                tan_secant(pair)
            for pair in range(PRODUCTS_AHEAD):
                tan_product(pair)
            for pair in range(LEAD):
                main_turns(pair)
                main_angles(pair)
            main_turns(LEAD)
            main_sines(0, 1, 1)
            finish(1)
            main_angles(LEAD)
            main_sines(0, 0, 0)
            finish(0)
            for pair in range(1, PAIRS):
                if pair + LEAD < PAIRS:
                    main_turns(pair + LEAD)
                    main_angles(pair + LEAD)
                if pair + 1 in SCALAR_LINEAR:
                    nc.scalar.copy(out=planes[:, pair + 1, LINEAR, :], in_=banks[pair + 1][1][:])
                main_sines(pair, 0, 1)
                for t in (pair * PAIR + 1, pair * PAIR) if pair < 5 else (pair * PAIR, pair * PAIR + 1):
                    finish(t)
                if pair + PRODUCTS_AHEAD - 1 < PAIRS:
                    tan_product(pair + PRODUCTS_AHEAD - 1)
